import numpy as np
import ml_dtypes


def mxq(x, axis, fmt="e4m3"):
    dtype, down = {"e4m3": (ml_dtypes.float8_e4m3fn, 7), "e5m2": (ml_dtypes.float8_e5m2, 14)}[fmt]
    v = np.moveaxis(np.asarray(x, np.float32).astype(ml_dtypes.bfloat16).astype(np.float64), axis, -1)
    blocks = v.reshape(v.shape[:-1] + (-1, 32))
    amax = np.abs(blocks).max(-1, keepdims=True)
    byte = np.maximum(np.where(amax > 0, np.frexp(amax)[1] - 1 + 127, 0) - down, 1)
    scale = np.exp2(byte - 127.0)
    codes = (blocks / scale).astype(np.float32).astype(dtype).astype(np.float64)
    return np.moveaxis((codes * scale).reshape(v.shape), -1, axis)


WIDE = False


def mx_kscale(k):
    if not WIDE:
        return np.ones(k)
    levels = np.array([18, -18])
    if k % 512:
        return np.exp2(np.random.permutation(np.resize(levels, k // 32))).repeat(32)
    a = np.empty((k // 512, 16))
    for p in range(k // 512):
        a[p, :8] = np.random.permutation(np.resize(levels, 8))
        for g in range(8):
            far = levels[np.abs(levels - a[p, g]) >= 10]
            a[p, g + 8] = far[np.random.randint(len(far))]
    return np.exp2(a.ravel()).repeat(32)


BF16 = ml_dtypes.bfloat16


def bf(x):
    return np.asarray(x, np.float32).astype(BF16)


def f64(x):
    return np.asarray(x).astype(np.float64)


B, D, S = 1024, 512, 1024
K1 = D + S
P = S // 2
EPS = 1e-6


def sigmoid(v):
    return 1.0 / (1.0 + np.exp(-v))


def cell_update(inputs, states, W1, b1, W2, b2, excitatory_potential, inhibitory_potential, capacitance,
                max_conductance, mean_conductance_potential, std_conductance):
    v = f64(states)
    b, n = v.shape
    cat = np.concatenate([f64(inputs), v], -1)
    h = cat @ f64(W1) + f64(b1)
    pre = h @ f64(W2) + f64(b2)
    m = np.stack([pre, -pre], -1).reshape(b, n)
    pairs = v.reshape(b, n // 2, 2)
    rolled = pairs[:, :, ::-1]
    presyn = np.concatenate([pairs, rolled], -1).reshape(b, n, 2)
    g = f64(max_conductance) * sigmoid(f64(std_conductance) * (presyn - f64(mean_conductance_potential)))
    rev = np.stack([f64(excitatory_potential), f64(inhibitory_potential)], -1)
    diff = rev - v[..., None]
    return v + (m + np.sum(g * diff, -1)) / f64(capacitance)


def norm_stats(xc):
    mu = np.mean(xc, -1, keepdims=True)
    var = np.mean((xc - mu) ** 2, -1, keepdims=True)
    return mu, 1.0 / np.sqrt(var + EPS)


def setup_inputs():
    r = np.random.standard_normal
    s = mx_kscale(B)[:, None]
    u = mx_kscale(P)
    v = mx_kscale(S)
    inputs0 = bf(r((B, D)))
    states0 = bf(r((B, S)))
    W1_0 = bf(r((K1, S)) / np.sqrt(K1))
    b1 = bf(r(S) * 0.2)
    W2_0 = bf(r((S, P)) / np.sqrt(S))
    b2 = bf(r(P) * 0.2)
    excitatory = bf(1.0 + 0.1 * r(S))
    inhibitory = bf(-1.0 + 0.1 * r(S))
    capacitance0 = bf(1.0 + 0.1 * r(S))
    max_c = bf(1.0 + 0.1 * r((S, 2)))
    mean_c = bf(0.3 * r((S, 2)))
    std_c = bf(1.0 + 0.2 * r((S, 2)))
    gamma = bf(1.0 + 0.1 * r(S))
    beta = bf(0.1 * r(S))
    g = bf(4.0 * r((B, S)) * np.exp2(np.random.randint(-6, 1, (B, 1))) / s)
    xc = cell_update(inputs0, states0, W1_0, b1, W2_0, b2, excitatory, inhibitory, capacitance0, max_c, mean_c, std_c)
    mu, rstd = norm_stats(xc)
    return {
        "inputs": bf(f64(inputs0) * s),
        "states": bf(f64(states0) * s),
        "W1": bf(f64(W1_0) / v),
        "b1": b1,
        "W2": bf(f64(W2_0) * v[:, None] / u),
        "b2": b2,
        "excitatory_potential": excitatory,
        "inhibitory_potential": inhibitory,
        "capacitance": bf(f64(capacitance0) / np.repeat(u, 2)),
        "max_conductance": max_c,
        "mean_conductance_potential": mean_c,
        "std_conductance": std_c,
        "gamma": gamma,
        "beta": beta,
        "x_new": np.asarray(xc, np.float32),
        "mu": np.asarray(mu, np.float32),
        "rstd": np.asarray(rstd, np.float32),
        "grad_out": g,
    }


def reference(inputs, states, W1, b1, W2, b2, excitatory_potential, inhibitory_potential, capacitance,
              max_conductance, mean_conductance_potential, std_conductance, gamma, beta, x_new, mu, rstd, grad_out):
    rs = f64(rstd)
    xhat = (f64(x_new) - f64(mu)) * rs
    dy = f64(grad_out) * f64(gamma)
    dxc = rs * (dy - np.mean(dy, -1, keepdims=True) - xhat * np.mean(dy * xhat, -1, keepdims=True))
    dm = dxc / f64(capacitance)
    dpre = dm[:, 0::2] - dm[:, 1::2]
    dh = mxq(dpre, 1, "e5m2") @ mxq(f64(W2), 1, "e4m3").T
    dinputs = mxq(dh, 1, "e5m2") @ mxq(f64(W1)[:D], 1, "e4m3").T
    cat = np.concatenate([f64(inputs), f64(states)], -1)
    dW1 = mxq(cat, 0, "e4m3").T @ mxq(dh, 0, "e5m2")
    return dinputs, dW1

@@ -1,0 +1,405 @@
+from contextlib import ExitStack
+
+import concourse.mybir as mybir
+from concourse.masks import make_identity
+
+B, D, S, P2 = 1024, 512, 1024, 512
+K1 = D + S
+FLOPS = 2 * (B * P2 * S + B * S * D + B * K1 * S)
+BYTES = 2 * (B * K1 + D * S + S * P2 + 2 * S + B * S) + 4 * (B * S + 2 * B) + 4 * (B * D + K1 * S)
+
+F32 = mybir.dt.float32
+BF16 = mybir.dt.bfloat16
+U32 = mybir.dt.uint32
+U8 = mybir.dt.uint8
+E4 = mybir.dt.float8_e4m3fn_x4
+E5 = mybir.dt.float8_e5m2_x4
+ALU = mybir.AluOpType
+ACT = mybir.ActivationFunctionType
+
+N = 128
+G = 2
+T = 4
+NT = G * T
+
+
+def tile_memorylayercell_pa_v_kernel(
+    tc, inputs, states, W1, b1, W2, b2, excitatory_potential, inhibitory_potential, capacitance,
+    max_conductance, mean_conductance_potential, std_conductance, gamma, beta, x_new, mu, rstd, grad_out,
+    out_0, out_1,
+):
+    nc = tc.nc
+    with ExitStack() as ctx:
+        keep = ctx.enter_context(tc.tile_pool(name="keep", bufs=1))
+        work = ctx.enter_context(tc.tile_pool(name="work", bufs=2))
+        psum = ctx.enter_context(tc.psum_pool(name="psum", bufs=2))
+        ctx.enter_context(tc.manual_schedule())
+
+        def ktile(shape, dtype, name):
+            return keep.tile(shape, dtype, name=name, tag=name, align_bytes=64)
+
+        def wtile(shape, dtype, tag, bufs=2):
+            return work.tile(shape, dtype, name=tag, tag=tag, bufs=bufs, align_bytes=64)
+
+        def bank(shape, tag):
+            return psum.tile(shape, F32, name=tag, tag=tag, bufs=2)
+
+        x_hbm = x_new.rearrange("(g p t) f -> g t p f", p=N, t=T)
+        g_hbm = grad_out.rearrange("(g p t) f -> g t p f", p=N, t=T)
+        xs, gs = {}, {}
+
+        def load_tok(i):
+            gs[i] = wtile([N, S], BF16, "g", 6)
+            nc.sync.dma_start(out=gs[i][:], in_=g_hbm[i // T, i % T])
+            xs[i] = wtile([N, S], F32, "x", 6)
+            nc.sync.dma_start(out=xs[i][:], in_=x_hbm[i // T, i % T])
+
+        gcol = ktile([N, 8], BF16, "gcol")
+        ccol = ktile([N, 8], BF16, "ccol")
+        mucol = ktile([N, NT], F32, "mucol")
+        rscol = ktile([N, NT], F32, "rscol")
+        nc.scalar.dma_start(out=gcol[:], in_=gamma.rearrange("(m q) -> m q", q=8))
+        nc.scalar.dma_start(out=rscol[:].rearrange("p (g t) -> p g t", t=T), in_=rstd.rearrange("(g p t) o -> p g (t o)", p=N, t=T))
+        nc.scalar.dma_start(out=mucol[:].rearrange("p (g t) -> p g t", t=T), in_=mu.rearrange("(g p t) o -> p g (t o)", p=N, t=T))
+        nc.scalar.dma_start(out=ccol[:], in_=capacitance.rearrange("(m q) -> m q", q=8))
+        load_tok(0)
+        w2raw = ktile([N, 8, P2], BF16, "w2raw")
+        w2_hbm = W2.rearrange("(b p) k -> p b k", p=N)
+        for h in range(2):
+            nc.sync.dma_start(out=w2raw[:, 4 * h:4 * h + 4, :], in_=w2_hbm[:, 4 * h:4 * h + 4, :])
+        load_tok(1)
+        catraw = {}
+
+        def load_cat(g):
+            catraw[g, 0] = ktile([N, T, D], BF16, "cat_i%d" % g)
+            nc.sync.dma_start(out=catraw[g, 0][:], in_=inputs.rearrange("(g p t) w -> g p t w", p=N, t=T)[g])
+            catraw[g, 1] = ktile([N, T, S], BF16, "cat_s%d" % g)
+            nc.sync.dma_start(out=catraw[g, 1][:], in_=states.rearrange("(g p t) w -> g p t w", p=N, t=T)[g])
+
+        load_tok(2)
+        w1raw = ktile([N, 4, S], BF16, "w1raw")
+        nc.sync.dma_start(out=w1raw[:], in_=W1[0:D, :].rearrange("(b p) k -> p b k", p=N))
+        load_cat(0)
+        load_tok(3)
+        load_tok(4)
+        load_cat(1)
+        load_tok(5)
+        load_tok(6)
+        load_tok(7)
+
+        warm = ktile([N, 1], F32, "warm")
+        nc.vector.memset(warm[:], 0.0)
+        nc.scalar.activation(out=warm[:], in_=warm[:], func=ACT.Identity, scale=1.0)
+        ident = ktile([N, N], F32, "ident")
+        make_identity(nc, ident[:])
+        identb = ktile([N, N], BF16, "identb")
+        nc.vector.tensor_copy(out=identb[:], in_=ident[:])
+        gam = ktile([N, 8, N], BF16, "gam")
+        for h in range(2):
+            gb = bank([N, 4, N], "mm")
+            for q in range(4):
+                j = 4 * h + q
+                nc.tensor.matmul(out=gb[:, q, :], lhsT=gcol[:, j:j + 1].to_broadcast([N, N]), rhs=identb[:], start=True, stop=True)
+            nc.scalar.copy(out=gam[:, 4 * h:4 * h + 4, :], in_=gb[:])
+        icol = ktile([N, 8], F32, "icol")
+        nicol = ktile([N, 8], F32, "nicol")
+        k2 = ktile([N, NT], F32, "k2")
+        k3 = ktile([N, NT], F32, "k3")
+        s1 = ktile([N, NT, 8], F32, "s1")
+        s2 = ktile([N, NT, 8], F32, "s2")
+        s1m = ktile([N, NT, 8], F32, "s1m")
+        na = ktile([N, NT, 8], F32, "na")
+        nb = ktile([N, NT, 8], F32, "nb")
+
+        dys, zs = {}, {}
+
+        def v1(i):
+            dys[i] = wtile([N, 8, N], F32, "dy", 3)
+            nc.vector.scalar_tensor_tensor(
+                out=dys[i][:], in0=gs[i][:].rearrange("p (m q) -> p q m", q=8), scalar=rscol[:, i:i + 1], in1=gam[:],
+                op0=ALU.mult, op1=ALU.mult, accum_out=s1[:, i, 0:1])
+            nc.gpsimd.tensor_scalar(s1m[:, i, 0:1], s1[:, i, 0:1], -1.0 / S, 0.0, ALU.mult, ALU.add)
+
+        def consts():
+            nc.vector.scalar_tensor_tensor(out=k2[:], in0=rscol[:], scalar=-1.0 / S, in1=rscol[:], op0=ALU.mult, op1=ALU.mult)
+            nc.vector.scalar_tensor_tensor(out=k3[:], in0=mucol[:], scalar=-1.0, in1=k2[:], op0=ALU.mult, op1=ALU.mult)
+            nc.vector.reciprocal(out=icol[:], in_=ccol[:])
+            nc.vector.tensor_scalar(nicol[:], icol[:], -1.0, None, ALU.mult)
+
+        def v2(i):
+            junk = wtile([N, 8, N], BF16, "junk", 2)
+            nc.vector.scalar_tensor_tensor(
+                out=junk[:], in0=xs[i][:].rearrange("p (m q) -> p q m", q=8), scalar=mucol[:, i:i + 1], in1=dys[i][:],
+                op0=ALU.subtract, op1=ALU.mult, accum_out=s2[:, i, 0:1])
+
+        def zz(i):
+            nc.scalar.activation(out=na[:, i, 0:1], in_=s2[:, i, 0:1], func=ACT.Copy, scale=k2[:, i:i + 1])
+            nc.scalar.activation(out=nb[:, i, 0:1], in_=s2[:, i, 0:1], func=ACT.Identity, scale=k3[:, i:i + 1], bias=s1m[:, i, 0:1])
+            zs[i] = wtile([N, 8, N], F32, "z", 2)
+            nc.scalar.activation(out=zs[i][:], in_=xs[i][:].rearrange("p (m q) -> p q m", q=8), func=ACT.Identity,
+                                 scale=na[:, i, 0:1], bias=nb[:, i, 0:1])
+
+        eb, ob, es = {}, {}, {}
+
+        def tr(i):
+            eb[i] = bank([N, T, N], "e")
+            ob[i] = bank([N, T, N], "o")
+            for e, dst in ((0, eb[i]), (1, ob[i])):
+                for t in range(T):
+                    nc.tensor.matmul(out=dst[:, t, :], lhsT=dys[i][:, 2 * t + e, :], rhs=ident[:], is_transpose=True, start=True, stop=False)
+                    nc.tensor.matmul(out=dst[:, t, :], lhsT=zs[i][:, 2 * t + e, :], rhs=ident[:], is_transpose=True, start=False, stop=True)
+
+        def esc(i):
+            es[i] = wtile([N, T, N], F32, "es", 2)
+            for t in range(T):
+                nc.scalar.activation(out=es[i][:, t, :], in_=eb[i][:, t, :], func=ACT.Copy, scale=icol[:, 2 * t:2 * t + 1])
+
+        dpc, dpi, dpq, dps = {}, {}, {}, {}
+
+        def comb(i):
+            dpc[i] = wtile([N, T, N], BF16, "dpc", 2)
+            for t in range(T):
+                nc.vector.scalar_tensor_tensor(out=dpc[i][:, t, :], in0=ob[i][:, t, :], scalar=nicol[:, 2 * t + 1:2 * t + 2], in1=es[i][:, t, :],
+                                               op0=ALU.mult, op1=ALU.add)
+
+        def interleave(eng, dst, src):
+            d = dst.rearrange("p (c i) t -> p c t i", i=4)
+            s = src.rearrange("p t (c i) -> p c t i", i=4)
+            if eng == "v":
+                nc.vector.tensor_copy(out=d, in_=s)
+            else:
+                nc.scalar.copy(out=d, in_=s)
+
+        def dpil(i):
+            dpi[i] = wtile([N, N, T], BF16, "dpi", 2)
+            interleave("v", dpi[i][:], dpc[i][:])
+
+        def quant(codes, scales, src, fmt):
+            nc.vector.quantize_mx(out=codes.bitcast(fmt), scales=scales, in_=src.rearrange("p c t -> p (c t)"))
+
+        def dpquant(i):
+            dpq[i] = wtile([N, N], U32, "dpq", 2)
+            dps[i] = wtile([N, N], U8, "dps", 2)
+            quant(dpq[i][:], dps[i][:], dpi[i][:], E5)
+
+        w2g = ktile([N, S, T], BF16, "w2g")
+        w2q = ktile([N, S], U32, "w2q")
+        w2s = ktile([N, S], U8, "w2s")
+
+        def w2tr(b):
+            wb = bank([N, 2, 2, N], "tr")
+            for bb in range(2):
+                words = w2raw[:, 2 * b + bb, :].bitcast(F32)
+                for u in range(2):
+                    nc.tensor.transpose(wb[:, bb, u, :], words[:, u::2], ident[:])
+            nc.scalar.copy(out=w2g[:, 256 * b:256 * b + 256, :].rearrange("p c t -> p (c t)").bitcast(F32).rearrange("p (b r u) -> p b r u", b=2, u=2),
+                           in_=wb[:].rearrange("p b u r -> p b r u"))
+
+        def w2quant(h):
+            quant(w2q[:, 512 * h:512 * h + 512], w2s[:, 512 * h:512 * h + 512], w2g[:, 512 * h:512 * h + 512, :], E4)
+
+        w1g = [ktile([N, D, T], BF16, "w1g%d" % q) for q in range(2)]
+        w1q = ktile([N, 2, D], U32, "w1q")
+        w1s = ktile([N, 2, D], U8, "w1s")
+
+        def w1tr(b):
+            wb = bank([N, 2, 2, N], "tr")
+            words = w1raw[:, b, :].bitcast(F32)
+            for q in range(2):
+                for u in range(2):
+                    nc.tensor.transpose(wb[:, q, u, :], words[:, 256 * q + u:256 * q + 256:2], ident[:])
+            for q in range(2):
+                nc.scalar.copy(out=w1g[q][:, N * b:N * b + N, :].rearrange("p c t -> p (c t)").bitcast(F32).rearrange("p (r u) -> p r u", u=2),
+                               in_=wb[:, q, :, :].rearrange("p u r -> p r u"))
+
+        def w1quant(q):
+            quant(w1q[:, q, :], w1s[:, q, :], w1g[q][:], E4)
+
+        mmb = {}
+        dhb = [ktile([N, T, S], BF16, "dhb%d" % g) for g in range(G)]
+
+        def mm(i, h):
+            mmb[i, h] = bank([N, 512], "mm")
+            nc.tensor.matmul_mx(out=mmb[i, h][:], lhsT=dpq[i][:].bitcast(E5), lhsT_scale=dps[i][:],
+                                rhs=w2q[:, 512 * h:512 * h + 512].bitcast(E4), rhs_scale=w2s[:, 512 * h:512 * h + 512], start=True, stop=True)
+
+        def ev(i, h, eng):
+            dst = dhb[i // T][:, i % T, 512 * h:512 * h + 512]
+            if eng == "v":
+                nc.vector.tensor_copy(out=dst, in_=mmb[i, h][:])
+            else:
+                nc.scalar.copy(out=dst, in_=mmb[i, h][:])
+
+        dtb, dtg, dtq, dts = {}, {}, {}, {}
+
+        def dtr(i):
+            dtb[i] = bank([N, 2, 2, N], "tr")
+            words = dhb[i // T][:, i % T, :].bitcast(F32)
+            for q in range(2):
+                for u in range(2):
+                    nc.tensor.transpose(dtb[i][:, q, u, :], words[:, 256 * q + u:256 * q + 256:2], ident[:])
+
+        def dcp(i, eng):
+            dtg[i] = wtile([N, 2 * N, T], BF16, "dtg", 2)
+            d = dtg[i][:].rearrange("p c t -> p (c t)").bitcast(F32).rearrange("p (q r u) -> p q r u", q=2, u=2)
+            s = dtb[i][:].rearrange("p q u r -> p q r u")
+            if eng == "v":
+                nc.vector.tensor_copy(out=d, in_=s)
+            else:
+                nc.scalar.copy(out=d, in_=s)
+
+        def dtquant(i):
+            dtq[i] = ktile([N, 2 * N], U32, "dtq%d" % i)
+            dts[i] = ktile([N, 2 * N], U8, "dts%d" % i)
+            quant(dtq[i][:], dts[i][:], dtg[i][:], E5)
+
+        def o0(i, eng):
+            acc = bank([N, 512], "mm")
+            for q in range(2):
+                cols = slice(N * q, N * q + N)
+                nc.tensor.matmul_mx(out=acc[:], lhsT=dtq[i][:, cols].bitcast(E5), lhsT_scale=dts[i][:, cols],
+                                    rhs=w1q[:, q, :].bitcast(E4), rhs_scale=w1s[:, q, :], start=(q == 0), stop=(q == 1))
+            st = wtile([N, 512], F32, "os", 10)
+            if eng == "v":
+                nc.vector.tensor_copy(out=st[:], in_=acc[:])
+            else:
+                nc.scalar.copy(out=st[:], in_=acc[:])
+            nc.sync.dma_start(out=out_0.rearrange("(g p t) d -> g t p d", p=N, t=T)[i // T, i % T], in_=st[:])
+
+        catq = ktile([N, G, K1], U32, "catq")
+        cats = ktile([N, G, K1], U8, "cats")
+        catg = {}
+
+        def cil(g, c, eng):
+            if c % 2 == 0:
+                catg[g, c // 2] = wtile([N, 512, T], BF16, "catg", 3)
+            part, c0 = (0, 256 * c) if c < 2 else (1, 256 * (c - 2))
+            interleave(eng, catg[g, c // 2][:, 256 * (c % 2):256 * (c % 2) + 256, :], catraw[g, part][:, :, c0:c0 + 256])
+
+        def cquant(g, c):
+            cols = slice(512 * c, 512 * c + 512)
+            quant(catq[:, g, cols], cats[:, g, cols], catg[g, c][:], E4)
+
+        dhi = {}
+        dhq = ktile([N, G, S], U32, "dhq")
+        dhs = ktile([N, G, S], U8, "dhs")
+
+        def hil(g, h, part, eng):
+            if part == 0:
+                dhi[g, h] = wtile([N, 512, T], BF16, "dhi", 2)
+            c0 = 512 * h + 256 * part
+            interleave(eng, dhi[g, h][:, 256 * part:256 * part + 256, :], dhb[g][:, :, c0:c0 + 256])
+
+        def hquant(g, h):
+            cols = slice(512 * h, 512 * h + 512)
+            quant(dhq[:, g, cols], dhs[:, g, cols], dhi[g, h][:], E5)
+
+        tags = ("e", "o", "tr", "mm")
+        state = {"n": 0}
+
+        oacc = {}
+
+        def o1mm(c, h, g):
+            if g == 0:
+                oacc[c, h] = bank([N, 512], tags[(12 * h + c) % 4])
+            nc.tensor.matmul_mx(out=oacc[c, h][:], lhsT=catq[:, g, N * c:N * c + N].bitcast(E4), lhsT_scale=cats[:, g, N * c:N * c + N],
+                                rhs=dhq[:, g, 512 * h:512 * h + 512].bitcast(E5), rhs_scale=dhs[:, g, 512 * h:512 * h + 512],
+                                start=(g == 0), stop=(g == 1))
+
+        def o1(c, h):
+            k = state["n"]
+            state["n"] = k + 1
+            if (c, h) not in oacc:
+                o1mm(c, h, 0)
+            o1mm(c, h, 1)
+            acc = oacc[c, h]
+            st = wtile([N, 512], F32, "os", 10)
+            if k % 2 == 0:
+                nc.vector.tensor_copy(out=st[:], in_=acc[:])
+            else:
+                nc.scalar.copy(out=st[:], in_=acc[:])
+            nc.sync.dma_start(out=out_1[N * c:N * c + N, 512 * h:512 * h + 512], in_=st[:])
+
+        v1(0)
+        consts()
+        v2(0)
+        for b in range(4):
+            w2tr(b)
+        zz(0)
+        tr(0)
+        v1(1)
+        w2quant(0)
+        v2(1)
+        w2quant(1)
+        esc(0)
+        v1(2)
+        s_chunks = {1: 1, 2: 1, 3: 1, 4: 1, 5: 1}
+        v_chunks = {1: 1, 2: 1, 3: 1, 5: 0, 6: 2, 7: 2}
+        chunks = [(g, c) for g in range(G) for c in range(6)]
+        pend = []
+
+        def take(eng):
+            g, c = chunks.pop(0)
+            cil(g, c, eng)
+            if c % 2 == 1:
+                pend.append((g, c // 2))
+
+        for k in range(NT):
+            if k + 1 < NT:
+                zz(k + 1)
+                tr(k + 1)
+            comb(k)
+            if k >= 2:
+                dtquant(k - 2)
+            dpil(k)
+            if k + 2 < NT:
+                v2(k + 2)
+            dpquant(k)
+            if k >= 1:
+                dcp(k - 1, "s")
+            for n in range(s_chunks.get(k, 0)):
+                take("s")
+            mm(k, 0)
+            mm(k, 1)
+            if k + 1 < NT:
+                esc(k + 1)
+            ev(k, 0, "s")
+            ev(k, 1, "s" if k < 7 else "v")
+            dtr(k)
+            if k in (1, 2):
+                w1tr(2 * (k - 1))
+                w1tr(2 * (k - 1) + 1)
+            if k in (3, 4):
+                w1quant(k - 3)
+            for n in range(v_chunks.get(k, 0)):
+                take("v")
+            while pend:
+                cquant(*pend.pop(0))
+            if k >= 4:
+                o0(k - 4, "s")
+            if k in (4, 5):
+                hil(0, k - 4, 0, "v")
+                hil(0, k - 4, 1, "v")
+            if k in (5, 6):
+                hquant(0, k - 5)
+            if k + 3 < NT:
+                v1(k + 3)
+        o0(4, "s")
+        for c in range(4):
+            o1mm(c, 0, 0)
+        hil(1, 0, 0, "v")
+        hil(1, 0, 1, "s")
+        dtquant(6)
+        hquant(1, 0)
+        hil(1, 1, 0, "v")
+        hil(1, 1, 1, "s")
+        o0(5, "s")
+        dcp(7, "s")
+        hquant(1, 1)
+        dtquant(7)
+        for n in range(12):
+            o1(n, 0)
+        for n in range(12):
+            o1(n, 1)
+            if n < 2:
+                o0(n + 6, "s" if n % 2 == 0 else "v")

@@ -54,11 +54,14 @@ def tile_memorylayercell_pa_v_kernel(
             xs[i] = wtile([N, S], F32, "x", 6)
             nc.sync.dma_start(out=xs[i][:], in_=x_hbm[i // T, i % T])
 
-        gcol = ktile([N, 8], BF16, "gcol")
+        ones = ktile([N, N], BF16, "ones")
+        nc.vector.memset(ones[:], 1.0)
+        grow = ktile([N, S], BF16, "grow")
+        nc.vector.memset(grow[:], 0.0)
         ccol = ktile([N, 8], BF16, "ccol")
         mucol = ktile([N, NT], F32, "mucol")
         rscol = ktile([N, NT], F32, "rscol")
-        nc.scalar.dma_start(out=gcol[:], in_=gamma.rearrange("(m q) -> m q", q=8))
+        nc.scalar.dma_start(out=grow[0:1, :], in_=gamma.unsqueeze(0))
         nc.scalar.dma_start(out=rscol[:].rearrange("p (g t) -> p g t", t=T), in_=rstd.rearrange("(g p t) o -> p g (t o)", p=N, t=T))
         nc.scalar.dma_start(out=mucol[:].rearrange("p (g t) -> p g t", t=T), in_=mu.rearrange("(g p t) o -> p g (t o)", p=N, t=T))
         nc.scalar.dma_start(out=ccol[:], in_=capacitance.rearrange("(m q) -> m q", q=8))
@@ -92,15 +95,14 @@ def tile_memorylayercell_pa_v_kernel(
         nc.scalar.activation(out=warm[:], in_=warm[:], func=ACT.Identity, scale=1.0)
         ident = ktile([N, N], F32, "ident")
         make_identity(nc, ident[:])
-        identb = ktile([N, N], BF16, "identb")
-        nc.vector.tensor_copy(out=identb[:], in_=ident[:])
-        gam = ktile([N, 8, N], BF16, "gam")
+        gam = ktile([N, S], BF16, "gam")
         for h in range(2):
-            gb = bank([N, 4, N], "mm")
-            for q in range(4):
-                j = 4 * h + q
-                nc.tensor.matmul(out=gb[:, q, :], lhsT=gcol[:, j:j + 1].to_broadcast([N, N]), rhs=identb[:], start=True, stop=True)
-            nc.scalar.copy(out=gam[:, 4 * h:4 * h + 4, :], in_=gb[:])
+            gb = bank([N, 512], "mm")
+            nc.tensor.matmul(out=gb[:], lhsT=ones[:], rhs=grow[:, 512 * h:512 * h + 512], start=True, stop=True)
+            if h == 0:
+                nc.scalar.copy(out=gam[:, 0:512], in_=gb[:])
+            else:
+                nc.vector.tensor_copy(out=gam[:, 512:1024], in_=gb[:])
         icol = ktile([N, 8], F32, "icol")
         nicol = ktile([N, 8], F32, "nicol")
         k2 = ktile([N, NT], F32, "k2")
@@ -114,9 +116,9 @@ def tile_memorylayercell_pa_v_kernel(
         dys, zs = {}, {}
 
         def v1(i):
-            dys[i] = wtile([N, 8, N], F32, "dy", 3)
+            dys[i] = wtile([N, S], F32, "dy", 3)
             nc.vector.scalar_tensor_tensor(
-                out=dys[i][:], in0=gs[i][:].rearrange("p (m q) -> p q m", q=8), scalar=rscol[:, i:i + 1], in1=gam[:],
+                out=dys[i][:], in0=gs[i][:], scalar=rscol[:, i:i + 1], in1=gam[:],
                 op0=ALU.mult, op1=ALU.mult, accum_out=s1[:, i, 0:1])
             nc.gpsimd.tensor_scalar(s1m[:, i, 0:1], s1[:, i, 0:1], -1.0 / S, 0.0, ALU.mult, ALU.add)
 
@@ -127,16 +129,16 @@ def tile_memorylayercell_pa_v_kernel(
             nc.vector.tensor_scalar(nicol[:], icol[:], -1.0, None, ALU.mult)
 
         def v2(i):
-            junk = wtile([N, 8, N], BF16, "junk", 2)
+            junk = wtile([N, S], BF16, "junk", 2)
             nc.vector.scalar_tensor_tensor(
-                out=junk[:], in0=xs[i][:].rearrange("p (m q) -> p q m", q=8), scalar=mucol[:, i:i + 1], in1=dys[i][:],
+                out=junk[:], in0=xs[i][:], scalar=mucol[:, i:i + 1], in1=dys[i][:],
                 op0=ALU.subtract, op1=ALU.mult, accum_out=s2[:, i, 0:1])
 
         def zz(i):
             nc.scalar.activation(out=na[:, i, 0:1], in_=s2[:, i, 0:1], func=ACT.Copy, scale=k2[:, i:i + 1])
             nc.scalar.activation(out=nb[:, i, 0:1], in_=s2[:, i, 0:1], func=ACT.Identity, scale=k3[:, i:i + 1], bias=s1m[:, i, 0:1])
-            zs[i] = wtile([N, 8, N], F32, "z", 2)
-            nc.scalar.activation(out=zs[i][:], in_=xs[i][:].rearrange("p (m q) -> p q m", q=8), func=ACT.Identity,
+            zs[i] = wtile([N, S], F32, "z", 2)
+            nc.scalar.activation(out=zs[i][:], in_=xs[i][:], func=ACT.Identity,
                                  scale=na[:, i, 0:1], bias=nb[:, i, 0:1])
 
         eb, ob, es = {}, {}, {}
@@ -146,8 +148,8 @@ def tile_memorylayercell_pa_v_kernel(
             ob[i] = bank([N, T, N], "o")
             for e, dst in ((0, eb[i]), (1, ob[i])):
                 for t in range(T):
-                    nc.tensor.matmul(out=dst[:, t, :], lhsT=dys[i][:, 2 * t + e, :], rhs=ident[:], is_transpose=True, start=True, stop=False)
-                    nc.tensor.matmul(out=dst[:, t, :], lhsT=zs[i][:, 2 * t + e, :], rhs=ident[:], is_transpose=True, start=False, stop=True)
+                    nc.tensor.matmul(out=dst[:, t, :], lhsT=dys[i][:, 2 * t + e::8], rhs=ident[:], is_transpose=True, start=True, stop=False)
+                    nc.tensor.matmul(out=dst[:, t, :], lhsT=zs[i][:, 2 * t + e::8], rhs=ident[:], is_transpose=True, start=False, stop=True)
 
         def esc(i):
             es[i] = wtile([N, T, N], F32, "es", 2)
@@ -349,6 +351,8 @@ def tile_memorylayercell_pa_v_kernel(
                 zz(k + 1)
                 tr(k + 1)
             comb(k)
+            while pend:
+                cquant(*pend.pop(0))
             if k >= 2:
                 dtquant(k - 2)
             dpil(k)
@@ -373,8 +377,6 @@ def tile_memorylayercell_pa_v_kernel(
                 w1quant(k - 3)
             for n in range(v_chunks.get(k, 0)):
                 take("v")
-            while pend:
-                cquant(*pend.pop(0))
             if k >= 4:
                 o0(k - 4, "s")
             if k in (4, 5):
@@ -384,6 +386,8 @@ def tile_memorylayercell_pa_v_kernel(
                 hquant(0, k - 5)
             if k + 3 < NT:
                 v1(k + 3)
+        while pend:
+            cquant(*pend.pop(0))
         o0(4, "s")
         for c in range(4):
             o1mm(c, 0, 0)

from contextlib import ExitStack

import concourse.mybir as mybir
from concourse.masks import make_identity

B, D, S, P2 = 1024, 512, 1024, 512
K1 = D + S
FLOPS = 2 * (B * P2 * S + B * S * D + B * K1 * S)
BYTES = 2 * (B * K1 + D * S + S * P2 + 2 * S + B * S) + 4 * (B * S + 2 * B) + 4 * (B * D + K1 * S)

F32 = mybir.dt.float32
BF16 = mybir.dt.bfloat16
U32 = mybir.dt.uint32
U8 = mybir.dt.uint8
E4 = mybir.dt.float8_e4m3fn_x4
E5 = mybir.dt.float8_e5m2_x4
ALU = mybir.AluOpType
ACT = mybir.ActivationFunctionType

N = 128
G = 2
T = 4
NT = G * T


def tile_memorylayercell_pa_v_kernel(
    tc, inputs, states, W1, b1, W2, b2, excitatory_potential, inhibitory_potential, capacitance,
    max_conductance, mean_conductance_potential, std_conductance, gamma, beta, x_new, mu, rstd, grad_out,
    out_0, out_1,
):
    nc = tc.nc
    with ExitStack() as ctx:
        keep = ctx.enter_context(tc.tile_pool(name="keep", bufs=1))
        work = ctx.enter_context(tc.tile_pool(name="work", bufs=2))
        psum = ctx.enter_context(tc.psum_pool(name="psum", bufs=2))
        ctx.enter_context(tc.manual_schedule())

        def ktile(shape, dtype, name):
            return keep.tile(shape, dtype, name=name, tag=name, align_bytes=64)

        def wtile(shape, dtype, tag, bufs=2):
            return work.tile(shape, dtype, name=tag, tag=tag, bufs=bufs, align_bytes=64)

        def bank(shape, tag):
            return psum.tile(shape, F32, name=tag, tag=tag, bufs=2)

        x_hbm = x_new.rearrange("(g p t) f -> g t p f", p=N, t=T)
        g_hbm = grad_out.rearrange("(g p t) f -> g t p f", p=N, t=T)
        xs, gs = {}, {}

        def load_tok(i):
            gs[i] = wtile([N, S], BF16, "g", 6)
            nc.sync.dma_start(out=gs[i][:], in_=g_hbm[i // T, i % T])
            xs[i] = wtile([N, S], F32, "x", 6)
            nc.sync.dma_start(out=xs[i][:], in_=x_hbm[i // T, i % T])

        ones = ktile([N, N], BF16, "ones")
        nc.vector.memset(ones[:], 1.0)
        grow = ktile([N, S], BF16, "grow")
        nc.vector.memset(grow[:], 0.0)
        ccol = ktile([N, 8], BF16, "ccol")
        mucol = ktile([N, NT], F32, "mucol")
        rscol = ktile([N, NT], F32, "rscol")
        nc.scalar.dma_start(out=grow[0:1, :], in_=gamma.unsqueeze(0))
        nc.scalar.dma_start(out=rscol[:].rearrange("p (g t) -> p g t", t=T), in_=rstd.rearrange("(g p t) o -> p g (t o)", p=N, t=T))
        nc.scalar.dma_start(out=mucol[:].rearrange("p (g t) -> p g t", t=T), in_=mu.rearrange("(g p t) o -> p g (t o)", p=N, t=T))
        nc.scalar.dma_start(out=ccol[:], in_=capacitance.rearrange("(m q) -> m q", q=8))
        load_tok(0)
        w2raw = ktile([N, 8, P2], BF16, "w2raw")
        w2_hbm = W2.rearrange("(b p) k -> p b k", p=N)
        for h in range(2):
            nc.sync.dma_start(out=w2raw[:, 4 * h:4 * h + 4, :], in_=w2_hbm[:, 4 * h:4 * h + 4, :])
        load_tok(1)
        catraw = {}

        def load_cat(g):
            catraw[g, 0] = ktile([N, T, D], BF16, "cat_i%d" % g)
            nc.sync.dma_start(out=catraw[g, 0][:], in_=inputs.rearrange("(g p t) w -> g p t w", p=N, t=T)[g])
            catraw[g, 1] = ktile([N, T, S], BF16, "cat_s%d" % g)
            nc.sync.dma_start(out=catraw[g, 1][:], in_=states.rearrange("(g p t) w -> g p t w", p=N, t=T)[g])

        load_tok(2)
        w1raw = ktile([N, 4, S], BF16, "w1raw")
        nc.sync.dma_start(out=w1raw[:], in_=W1[0:D, :].rearrange("(b p) k -> p b k", p=N))
        load_cat(0)
        load_tok(3)
        load_tok(4)
        load_cat(1)
        load_tok(5)
        load_tok(6)
        load_tok(7)

        warm = ktile([N, 1], F32, "warm")
        nc.vector.memset(warm[:], 0.0)
        nc.scalar.activation(out=warm[:], in_=warm[:], func=ACT.Identity, scale=1.0)
        ident = ktile([N, N], F32, "ident")
        make_identity(nc, ident[:])
        gam = ktile([N, S], BF16, "gam")
        for h in range(2):
            gb = bank([N, 512], "mm")
            nc.tensor.matmul(out=gb[:], lhsT=ones[:], rhs=grow[:, 512 * h:512 * h + 512], start=True, stop=True)
            if h == 0:
                nc.scalar.copy(out=gam[:, 0:512], in_=gb[:])
            else:
                nc.vector.tensor_copy(out=gam[:, 512:1024], in_=gb[:])
        icol = ktile([N, 8], F32, "icol")
        nicol = ktile([N, 8], F32, "nicol")
        k2 = ktile([N, NT], F32, "k2")
        k3 = ktile([N, NT], F32, "k3")
        s1 = ktile([N, NT, 8], F32, "s1")
        s2 = ktile([N, NT, 8], F32, "s2")
        s1m = ktile([N, NT, 8], F32, "s1m")
        na = ktile([N, NT, 8], F32, "na")
        nb = ktile([N, NT, 8], F32, "nb")

        dys, zs = {}, {}

        def v1(i):
            dys[i] = wtile([N, S], F32, "dy", 3)
            nc.vector.scalar_tensor_tensor(
                out=dys[i][:], in0=gs[i][:], scalar=rscol[:, i:i + 1], in1=gam[:],
                op0=ALU.mult, op1=ALU.mult, accum_out=s1[:, i, 0:1])
            nc.gpsimd.tensor_scalar(s1m[:, i, 0:1], s1[:, i, 0:1], -1.0 / S, 0.0, ALU.mult, ALU.add)

        def consts():
            nc.vector.scalar_tensor_tensor(out=k2[:], in0=rscol[:], scalar=-1.0 / S, in1=rscol[:], op0=ALU.mult, op1=ALU.mult)
            nc.vector.scalar_tensor_tensor(out=k3[:], in0=mucol[:], scalar=-1.0, in1=k2[:], op0=ALU.mult, op1=ALU.mult)
            nc.vector.reciprocal(out=icol[:], in_=ccol[:])
            nc.vector.tensor_scalar(nicol[:], icol[:], -1.0, None, ALU.mult)

        def v2(i):
            junk = wtile([N, S], BF16, "junk", 2)
            nc.vector.scalar_tensor_tensor(
                out=junk[:], in0=xs[i][:], scalar=mucol[:, i:i + 1], in1=dys[i][:],
                op0=ALU.subtract, op1=ALU.mult, accum_out=s2[:, i, 0:1])

        def zz(i):
            nc.scalar.activation(out=na[:, i, 0:1], in_=s2[:, i, 0:1], func=ACT.Copy, scale=k2[:, i:i + 1])
            nc.scalar.activation(out=nb[:, i, 0:1], in_=s2[:, i, 0:1], func=ACT.Identity, scale=k3[:, i:i + 1], bias=s1m[:, i, 0:1])
            zs[i] = wtile([N, S], F32, "z", 2)
            nc.scalar.activation(out=zs[i][:], in_=xs[i][:], func=ACT.Identity,
                                 scale=na[:, i, 0:1], bias=nb[:, i, 0:1])

        eb, ob, es = {}, {}, {}

        def tr(i):
            eb[i] = bank([N, T, N], "e")
            ob[i] = bank([N, T, N], "o")
            for e, dst in ((0, eb[i]), (1, ob[i])):
                for t in range(T):
                    nc.tensor.matmul(out=dst[:, t, :], lhsT=dys[i][:, 2 * t + e::8], rhs=ident[:], is_transpose=True, start=True, stop=False)
                    nc.tensor.matmul(out=dst[:, t, :], lhsT=zs[i][:, 2 * t + e::8], rhs=ident[:], is_transpose=True, start=False, stop=True)

        def esc(i):
            es[i] = wtile([N, T, N], F32, "es", 2)
            for t in range(T):
                nc.scalar.activation(out=es[i][:, t, :], in_=eb[i][:, t, :], func=ACT.Copy, scale=icol[:, 2 * t:2 * t + 1])

        dpc, dpi, dpq, dps = {}, {}, {}, {}

        def comb(i):
            dpc[i] = wtile([N, T, N], BF16, "dpc", 2)
            for t in range(T):
                nc.vector.scalar_tensor_tensor(out=dpc[i][:, t, :], in0=ob[i][:, t, :], scalar=nicol[:, 2 * t + 1:2 * t + 2], in1=es[i][:, t, :],
                                               op0=ALU.mult, op1=ALU.add)

        def interleave(eng, dst, src):
            d = dst.rearrange("p (c i) t -> p c t i", i=4)
            s = src.rearrange("p t (c i) -> p c t i", i=4)
            if eng == "v":
                nc.vector.tensor_copy(out=d, in_=s)
            else:
                nc.scalar.copy(out=d, in_=s)

        def dpil(i):
            dpi[i] = wtile([N, N, T], BF16, "dpi", 2)
            interleave("v", dpi[i][:], dpc[i][:])

        def quant(codes, scales, src, fmt):
            nc.vector.quantize_mx(out=codes.bitcast(fmt), scales=scales, in_=src.rearrange("p c t -> p (c t)"))

        def dpquant(i):
            dpq[i] = wtile([N, N], U32, "dpq", 2)
            dps[i] = wtile([N, N], U8, "dps", 2)
            quant(dpq[i][:], dps[i][:], dpi[i][:], E5)

        w2g = ktile([N, S, T], BF16, "w2g")
        w2q = ktile([N, S], U32, "w2q")
        w2s = ktile([N, S], U8, "w2s")

        def w2tr(b):
            wb = bank([N, 2, 2, N], "tr")
            for bb in range(2):
                words = w2raw[:, 2 * b + bb, :].bitcast(F32)
                for u in range(2):
                    nc.tensor.transpose(wb[:, bb, u, :], words[:, u::2], ident[:])
            nc.scalar.copy(out=w2g[:, 256 * b:256 * b + 256, :].rearrange("p c t -> p (c t)").bitcast(F32).rearrange("p (b r u) -> p b r u", b=2, u=2),
                           in_=wb[:].rearrange("p b u r -> p b r u"))

        def w2quant(h):
            quant(w2q[:, 512 * h:512 * h + 512], w2s[:, 512 * h:512 * h + 512], w2g[:, 512 * h:512 * h + 512, :], E4)

        w1g = [ktile([N, D, T], BF16, "w1g%d" % q) for q in range(2)]
        w1q = ktile([N, 2, D], U32, "w1q")
        w1s = ktile([N, 2, D], U8, "w1s")

        def w1tr(b):
            wb = bank([N, 2, 2, N], "tr")
            words = w1raw[:, b, :].bitcast(F32)
            for q in range(2):
                for u in range(2):
                    nc.tensor.transpose(wb[:, q, u, :], words[:, 256 * q + u:256 * q + 256:2], ident[:])
            for q in range(2):
                nc.scalar.copy(out=w1g[q][:, N * b:N * b + N, :].rearrange("p c t -> p (c t)").bitcast(F32).rearrange("p (r u) -> p r u", u=2),
                               in_=wb[:, q, :, :].rearrange("p u r -> p r u"))

        def w1quant(q):
            quant(w1q[:, q, :], w1s[:, q, :], w1g[q][:], E4)

        mmb = {}
        dhb = [ktile([N, T, S], BF16, "dhb%d" % g) for g in range(G)]

        def mm(i, h):
            mmb[i, h] = bank([N, 512], "mm")
            nc.tensor.matmul_mx(out=mmb[i, h][:], lhsT=dpq[i][:].bitcast(E5), lhsT_scale=dps[i][:],
                                rhs=w2q[:, 512 * h:512 * h + 512].bitcast(E4), rhs_scale=w2s[:, 512 * h:512 * h + 512], start=True, stop=True)

        def ev(i, h, eng):
            dst = dhb[i // T][:, i % T, 512 * h:512 * h + 512]
            if eng == "v":
                nc.vector.tensor_copy(out=dst, in_=mmb[i, h][:])
            else:
                nc.scalar.copy(out=dst, in_=mmb[i, h][:])

        dtb, dtg, dtq, dts = {}, {}, {}, {}

        def dtr(i):
            dtb[i] = bank([N, 2, 2, N], "tr")
            words = dhb[i // T][:, i % T, :].bitcast(F32)
            for q in range(2):
                for u in range(2):
                    nc.tensor.transpose(dtb[i][:, q, u, :], words[:, 256 * q + u:256 * q + 256:2], ident[:])

        def dcp(i, eng):
            dtg[i] = wtile([N, 2 * N, T], BF16, "dtg", 2)
            d = dtg[i][:].rearrange("p c t -> p (c t)").bitcast(F32).rearrange("p (q r u) -> p q r u", q=2, u=2)
            s = dtb[i][:].rearrange("p q u r -> p q r u")
            if eng == "v":
                nc.vector.tensor_copy(out=d, in_=s)
            else:
                nc.scalar.copy(out=d, in_=s)

        def dtquant(i):
            dtq[i] = ktile([N, 2 * N], U32, "dtq%d" % i)
            dts[i] = ktile([N, 2 * N], U8, "dts%d" % i)
            quant(dtq[i][:], dts[i][:], dtg[i][:], E5)

        def o0(i, eng):
            acc = bank([N, 512], "mm")
            for q in range(2):
                cols = slice(N * q, N * q + N)
                nc.tensor.matmul_mx(out=acc[:], lhsT=dtq[i][:, cols].bitcast(E5), lhsT_scale=dts[i][:, cols],
                                    rhs=w1q[:, q, :].bitcast(E4), rhs_scale=w1s[:, q, :], start=(q == 0), stop=(q == 1))
            st = wtile([N, 512], F32, "os", 10)
            if eng == "v":
                nc.vector.tensor_copy(out=st[:], in_=acc[:])
            else:
                nc.scalar.copy(out=st[:], in_=acc[:])
            nc.sync.dma_start(out=out_0.rearrange("(g p t) d -> g t p d", p=N, t=T)[i // T, i % T], in_=st[:])

        catq = ktile([N, G, K1], U32, "catq")
        cats = ktile([N, G, K1], U8, "cats")
        catg = {}

        def cil(g, c, eng):
            if c % 2 == 0:
                catg[g, c // 2] = wtile([N, 512, T], BF16, "catg", 3)
            part, c0 = (0, 256 * c) if c < 2 else (1, 256 * (c - 2))
            interleave(eng, catg[g, c // 2][:, 256 * (c % 2):256 * (c % 2) + 256, :], catraw[g, part][:, :, c0:c0 + 256])

        def cquant(g, c):
            cols = slice(512 * c, 512 * c + 512)
            quant(catq[:, g, cols], cats[:, g, cols], catg[g, c][:], E4)

        dhi = {}
        dhq = ktile([N, G, S], U32, "dhq")
        dhs = ktile([N, G, S], U8, "dhs")

        def hil(g, h, part, eng):
            if part == 0:
                dhi[g, h] = wtile([N, 512, T], BF16, "dhi", 2)
            c0 = 512 * h + 256 * part
            interleave(eng, dhi[g, h][:, 256 * part:256 * part + 256, :], dhb[g][:, :, c0:c0 + 256])

        def hquant(g, h):
            cols = slice(512 * h, 512 * h + 512)
            quant(dhq[:, g, cols], dhs[:, g, cols], dhi[g, h][:], E5)

        tags = ("e", "o", "tr", "mm")
        state = {"n": 0}

        oacc = {}

        def o1mm(c, h, g):
            if g == 0:
                oacc[c, h] = bank([N, 512], tags[(12 * h + c) % 4])
            nc.tensor.matmul_mx(out=oacc[c, h][:], lhsT=catq[:, g, N * c:N * c + N].bitcast(E4), lhsT_scale=cats[:, g, N * c:N * c + N],
                                rhs=dhq[:, g, 512 * h:512 * h + 512].bitcast(E5), rhs_scale=dhs[:, g, 512 * h:512 * h + 512],
                                start=(g == 0), stop=(g == 1))

        def o1(c, h):
            k = state["n"]
            state["n"] = k + 1
            if (c, h) not in oacc:
                o1mm(c, h, 0)
            o1mm(c, h, 1)
            acc = oacc[c, h]
            st = wtile([N, 512], F32, "os", 10)
            if k % 2 == 0:
                nc.vector.tensor_copy(out=st[:], in_=acc[:])
            else:
                nc.scalar.copy(out=st[:], in_=acc[:])
            nc.sync.dma_start(out=out_1[N * c:N * c + N, 512 * h:512 * h + 512], in_=st[:])

        v1(0)
        consts()
        v2(0)
        for b in range(4):
            w2tr(b)
        zz(0)
        tr(0)
        v1(1)
        w2quant(0)
        v2(1)
        w2quant(1)
        esc(0)
        v1(2)
        s_chunks = {1: 1, 2: 1, 3: 1, 4: 1, 5: 1}
        v_chunks = {1: 1, 2: 1, 3: 1, 5: 0, 6: 2, 7: 2}
        chunks = [(g, c) for g in range(G) for c in range(6)]
        pend = []

        def take(eng):
            g, c = chunks.pop(0)
            cil(g, c, eng)
            if c % 2 == 1:
                pend.append((g, c // 2))

        for k in range(NT):
            if k + 1 < NT:
                zz(k + 1)
                tr(k + 1)
            comb(k)
            while pend:
                cquant(*pend.pop(0))
            if k >= 2:
                dtquant(k - 2)
            dpil(k)
            if k + 2 < NT:
                v2(k + 2)
            dpquant(k)
            if k >= 1:
                dcp(k - 1, "s")
            for n in range(s_chunks.get(k, 0)):
                take("s")
            mm(k, 0)
            mm(k, 1)
            if k + 1 < NT:
                esc(k + 1)
            ev(k, 0, "s")
            ev(k, 1, "s" if k < 7 else "v")
            dtr(k)
            if k in (1, 2):
                w1tr(2 * (k - 1))
                w1tr(2 * (k - 1) + 1)
            if k in (3, 4):
                w1quant(k - 3)
            for n in range(v_chunks.get(k, 0)):
                take("v")
            if k >= 4:
                o0(k - 4, "s")
            if k in (4, 5):
                hil(0, k - 4, 0, "v")
                hil(0, k - 4, 1, "v")
            if k in (5, 6):
                hquant(0, k - 5)
            if k + 3 < NT:
                v1(k + 3)
        while pend:
            cquant(*pend.pop(0))
        o0(4, "s")
        for c in range(4):
            o1mm(c, 0, 0)
        hil(1, 0, 0, "v")
        hil(1, 0, 1, "s")
        dtquant(6)
        hquant(1, 0)
        hil(1, 1, 0, "v")
        hil(1, 1, 1, "s")
        o0(5, "s")
        dcp(7, "s")
        hquant(1, 1)
        dtquant(7)
        for n in range(12):
            o1(n, 0)
        for n in range(12):
            o1(n, 1)
            if n < 2:
                o0(n + 6, "s" if n % 2 == 0 else "v")
